import numpy as np
import ml_dtypes


def mxq(x, axis, fmt="e4m3"):
    dtype, down = {"e4m3": (ml_dtypes.float8_e4m3fn, 7), "e5m2": (ml_dtypes.float8_e5m2, 14)}[fmt]
    v = np.moveaxis(np.asarray(x, np.float32).astype(ml_dtypes.bfloat16).astype(np.float64), axis, -1)
    blocks = v.reshape(v.shape[:-1] + (-1, 32))
    amax = np.abs(blocks).max(-1, keepdims=True)
    byte = np.maximum(np.where(amax > 0, np.frexp(amax)[1] - 1 + 127, 0) - down, 1)
    scale = np.exp2(byte - 127.0)
    codes = (blocks / scale).astype(np.float32).astype(dtype).astype(np.float64)
    return np.moveaxis((codes * scale).reshape(v.shape), -1, axis)


WIDE = False


def mx_kscale(k):
    if not WIDE:
        return np.ones(k)
    levels = np.array([20, -20, 10, -10, 0])
    a = np.random.permutation(np.resize(levels, k // 512 * 4)).reshape(k // 512, 4)
    idx = np.arange(k)
    return np.exp2(a[idx // 512, idx % 128 // 32])


BF16 = ml_dtypes.bfloat16


def bf(x):
    return np.asarray(x, np.float32).astype(BF16)


def f64(x):
    return np.asarray(x).astype(np.float64)


B, S, D, BD, K = 2, 1024, 1024, 512, 128
T = B * S
TS = 3.0


def sigmoid(v):
    return 1.0 / (1.0 + np.exp(-v))


def setup_inputs():
    s = mx_kscale(T).reshape(B, S, 1)
    x0 = bf(np.random.standard_normal((B, S, D)) * TS)
    si = bf(np.random.uniform(size=(B, S, K)))
    dec = bf(np.random.standard_normal((B, K, D)) * 0.35)
    w = bf(np.random.standard_normal((D, D)) / (TS * np.sqrt(D)))
    b = bf(np.random.standard_normal(D) * 0.5)
    g = bf(np.random.standard_normal((B, S, D)) * np.exp2(np.random.randint(-12, 1, (B, S, 1))) / s)
    flow = f64(si) @ f64(dec)
    gate = sigmoid(f64(x0) @ f64(w) + f64(b))
    return {
        "token_embeddings": bf(f64(x0) * s),
        "splat_influences": si,
        "decoded": dec,
        "gate_W": w,
        "gate_b": b,
        "flow": np.asarray(flow, np.float32),
        "gate": np.asarray(gate, np.float32),
        "grad_out": g,
    }


def reference(token_embeddings, splat_influences, decoded, gate_W, gate_b, flow, gate, grad_out):
    x = f64(token_embeddings).reshape(T, D)
    gt = f64(gate)
    dz = (f64(grad_out) * f64(flow) * gt * (1.0 - gt)).reshape(T, D)
    return mxq(x, 0, "e4m3").T @ mxq(dz, 0, "e5m2")

@@ -1,0 +1,161 @@
+from contextlib import ExitStack
+
+import concourse.mybir as mybir
+
+F32 = mybir.dt.float32
+BF16 = mybir.dt.bfloat16
+U32 = mybir.dt.uint32
+U8 = mybir.dt.uint8
+E4M3_X4 = mybir.dt.float8_e4m3fn_x4
+E5M2_X4 = mybir.dt.float8_e5m2_x4
+ALU = mybir.AluOpType
+
+P = 128
+PACK = 4
+K_PASS = P * PACK
+TOKENS = 2048
+FEATURES = 1024
+PASSES = TOKENS // K_PASS
+M_TILE = 128
+N_TILE = 512
+M_TILES = FEATURES // M_TILE
+N_TILES = FEATURES // N_TILE
+LAST_GROUP = 2
+FETCH_AHEAD = 2
+X_LAG = 2
+RUN = 4
+
+FLOPS = 2 * TOKENS * FEATURES * FEATURES
+BYTES = TOKENS * FEATURES * (2 + 2 + 4 + 4) + FEATURES * FEATURES * 4
+
+
+def by_token(rows_cols):
+    return rows_cols.rearrange("p t (c i) -> p c t i", i=RUN)
+
+
+def by_column(cols_rows):
+    return cols_rows.rearrange("p (c i) t -> p c t i", i=RUN)
+
+
+def tile_splatinformationflow_pb_v_kernel(
+    tc, token_embeddings, splat_influences, decoded, gate_W, gate_b, flow, gate, grad_out, out
+):
+    nc = tc.nc
+
+    def chunk_of(tensor, c):
+        rows = tensor.rearrange("b s d -> (b s) d")[c * K_PASS : (c + 1) * K_PASS, :]
+        return rows.rearrange("(p t) w -> p t w", t=PACK)
+
+    groups = [[c] for c in range(PASSES - LAST_GROUP)] + [list(range(PASSES - LAST_GROUP, PASSES))]
+    units = [(c, n) for group in groups for n in range(N_TILES) for c in group]
+    last_of_round_0 = units.index((PASSES - 1, 0))
+
+    with ExitStack() as ctx:
+        ctx.enter_context(tc.manual_schedule())
+        keep = ctx.enter_context(tc.tile_pool(name="keep", bufs=1))
+        stream = ctx.enter_context(tc.tile_pool(name="stream", bufs=6))
+        x_stream = ctx.enter_context(tc.tile_pool(name="x_stream", bufs=2))
+        grouped = ctx.enter_context(tc.tile_pool(name="grouped", bufs=2))
+        results = ctx.enter_context(tc.tile_pool(name="results", bufs=M_TILES))
+        psum = ctx.enter_context(tc.psum_pool(name="psum", bufs=M_TILES))
+
+        x_codes = keep.tile([P, PASSES, FEATURES], U32, align_bytes=64)
+        x_scales = keep.tile([P, PASSES, FEATURES], U8, align_bytes=64)
+        dz_codes = keep.tile([P, PASSES, FEATURES], U32, align_bytes=64)
+        dz_scales = keep.tile([P, PASSES, FEATURES], U8, align_bytes=64)
+
+        inputs = {}
+        x_grouped = {}
+
+        def fetch(i):
+            c, n = units[i]
+            n_cols = slice(n * N_TILE, (n + 1) * N_TILE)
+            gate_t = stream.tile([P, PACK, N_TILE], F32)
+            nc.sync.dma_start(out=gate_t[:], in_=chunk_of(gate, c)[:, :, n_cols])
+            grad_t = stream.tile([P, PACK, N_TILE], BF16)
+            nc.sync.dma_start(out=grad_t[:], in_=chunk_of(grad_out, c)[:, :, n_cols])
+            flow_t = stream.tile([P, PACK, N_TILE], F32)
+            nc.sync.dma_start(out=flow_t[:], in_=chunk_of(flow, c)[:, :, n_cols])
+            inputs[i] = (gate_t, grad_t, flow_t)
+            if 0 <= i - 1 < PASSES:
+                x_t = x_stream.tile([P, PACK, FEATURES], BF16)
+                nc.sync.dma_start(out=x_t[:], in_=chunk_of(token_embeddings, i - 1))
+                x_g = x_stream.tile([P, FEATURES, PACK], BF16, align_bytes=64)
+                nc.scalar.copy(out=by_column(x_g[:]), in_=by_token(x_t[:]))
+                x_grouped[i - 1] = x_g
+
+        def gate_slope(i):
+            gate_t = inputs[i][0]
+            nc.vector.scalar_tensor_tensor(
+                out=gate_t[:], in0=gate_t[:], scalar=1.0, in1=gate_t[:], op0=ALU.subtract, op1=ALU.mult
+            )
+
+        def multiply(banks, c, n):
+            n_cols = slice(n * N_TILE, (n + 1) * N_TILE)
+            for m in range(M_TILES):
+                m_cols = slice(m * M_TILE, (m + 1) * M_TILE)
+                nc.tensor.matmul_mx(
+                    out=banks[m][:],
+                    lhsT=x_codes[:, c, m_cols].bitcast(E4M3_X4),
+                    lhsT_scale=x_scales[:, c, m_cols],
+                    rhs=dz_codes[:, c, n_cols].bitcast(E5M2_X4),
+                    rhs_scale=dz_scales[:, c, n_cols],
+                    start=(c == 0),
+                    stop=(c == PASSES - 1),
+                )
+
+        def store(bank, m, n, copy):
+            result = results.tile([M_TILE, N_TILE], F32)
+            copy(out=result[:], in_=bank[:])
+            nc.sync.dma_start(
+                out=out[m * M_TILE : (m + 1) * M_TILE, n * N_TILE : (n + 1) * N_TILE], in_=result[:]
+            )
+
+        round_0 = [psum.tile([M_TILE, N_TILE], F32, name="bank%d" % m, tag="bank") for m in range(M_TILES)]
+        round_1 = []
+        waiting = []
+
+        for i in range(FETCH_AHEAD):
+            fetch(i)
+        gate_slope(0)
+
+        for i, (c, n) in enumerate(units):
+            if i + FETCH_AHEAD < len(units):
+                fetch(i + FETCH_AHEAD)
+            gate_t, grad_t, flow_t = inputs[i]
+            n_cols = slice(n * N_TILE, (n + 1) * N_TILE)
+            nc.vector.scalar_tensor_tensor(
+                out=flow_t[:], in0=grad_t[:], scalar=-1.0, in1=flow_t[:], op0=ALU.mult, op1=ALU.mult
+            )
+            dz_grouped = grouped.tile([P, N_TILE, PACK], BF16, align_bytes=64)
+            nc.vector.tensor_tensor(
+                out=by_column(dz_grouped[:]), in0=by_token(gate_t[:]), in1=by_token(flow_t[:]), op=ALU.mult
+            )
+            if i + 1 < len(units):
+                gate_slope(i + 1)
+            x_chunk = i - X_LAG
+            if 0 <= x_chunk < PASSES:
+                nc.vector.quantize_mx(
+                    out=x_codes[:, x_chunk, :].bitcast(E4M3_X4), scales=x_scales[:, x_chunk, :],
+                    in_=x_grouped[x_chunk][:].rearrange("p w t -> p (w t)"),
+                )
+            nc.vector.quantize_mx(
+                out=dz_codes[:, c, n_cols].bitcast(E5M2_X4), scales=dz_scales[:, c, n_cols],
+                in_=dz_grouped[:].rearrange("p w t -> p (w t)"),
+            )
+
+            if 0 <= x_chunk < PASSES:
+                multiply(round_0, x_chunk, 0)
+            if n == 1:
+                waiting.append(c)
+            if i == last_of_round_0:
+                for m in range(M_TILES):
+                    store(round_0[m], m, 0, nc.scalar.copy)
+                    round_1.append(psum.tile([M_TILE, N_TILE], F32, name="bank%d" % (M_TILES + m), tag="bank"))
+            if i >= last_of_round_0:
+                for ready in waiting:
+                    multiply(round_1, ready, 1)
+                waiting = []
+
+        for m in range(M_TILES):
+            store(round_1[m], m, 1, nc.scalar.copy if m % 2 == 0 else nc.vector.tensor_copy)

@@ -22,7 +22,8 @@ M_TILES = FEATURES // M_TILE
 N_TILES = FEATURES // N_TILE
 LAST_GROUP = 2
 FETCH_AHEAD = 2
-X_LAG = 2
+X_LAG = 3
+HEAD_PIECES = 2
 RUN = 4
 
 FLOPS = 2 * TOKENS * FEATURES * FEATURES
@@ -48,7 +49,7 @@ def tile_splatinformationflow_pb_v_kernel(
 
     groups = [[c] for c in range(PASSES - LAST_GROUP)] + [list(range(PASSES - LAST_GROUP, PASSES))]
     units = [(c, n) for group in groups for n in range(N_TILES) for c in group]
-    last_of_round_0 = units.index((PASSES - 1, 0))
+    assert all(units.index((c, 0)) + 1 <= c + X_LAG for c in range(PASSES))
 
     with ExitStack() as ctx:
         ctx.enter_context(tc.manual_schedule())
@@ -66,17 +67,25 @@ def tile_splatinformationflow_pb_v_kernel(
 
         inputs = {}
         x_grouped = {}
+        dz_grouped = {}
+
+        def pieces_of(i):
+            pieces = HEAD_PIECES if i == 0 else 1
+            width = N_TILE // pieces
+            return [(k * width, (k + 1) * width) for k in range(pieces)]
 
         def fetch(i):
             c, n = units[i]
-            n_cols = slice(n * N_TILE, (n + 1) * N_TILE)
             gate_t = stream.tile([P, PACK, N_TILE], F32)
-            nc.sync.dma_start(out=gate_t[:], in_=chunk_of(gate, c)[:, :, n_cols])
             grad_t = stream.tile([P, PACK, N_TILE], BF16)
-            nc.sync.dma_start(out=grad_t[:], in_=chunk_of(grad_out, c)[:, :, n_cols])
             flow_t = stream.tile([P, PACK, N_TILE], F32)
-            nc.sync.dma_start(out=flow_t[:], in_=chunk_of(flow, c)[:, :, n_cols])
             inputs[i] = (gate_t, grad_t, flow_t)
+            for lo, hi in pieces_of(i):
+                cols = slice(lo, hi)
+                dram_cols = slice(n * N_TILE + lo, n * N_TILE + hi)
+                nc.sync.dma_start(out=gate_t[:, :, cols], in_=chunk_of(gate, c)[:, :, dram_cols])
+                nc.sync.dma_start(out=grad_t[:, :, cols], in_=chunk_of(grad_out, c)[:, :, dram_cols])
+                nc.sync.dma_start(out=flow_t[:, :, cols], in_=chunk_of(flow, c)[:, :, dram_cols])
             if 0 <= i - 1 < PASSES:
                 x_t = x_stream.tile([P, PACK, FEATURES], BF16)
                 nc.sync.dma_start(out=x_t[:], in_=chunk_of(token_embeddings, i - 1))
@@ -84,10 +93,39 @@ def tile_splatinformationflow_pb_v_kernel(
                 nc.scalar.copy(out=by_column(x_g[:]), in_=by_token(x_t[:]))
                 x_grouped[i - 1] = x_g
 
-        def gate_slope(i):
-            gate_t = inputs[i][0]
-            nc.vector.scalar_tensor_tensor(
-                out=gate_t[:], in0=gate_t[:], scalar=1.0, in1=gate_t[:], op0=ALU.subtract, op1=ALU.mult
+        def make_factors(i):
+            gate_t, grad_t, flow_t = inputs[i]
+            for lo, hi in pieces_of(i):
+                cols = slice(lo, hi)
+                nc.vector.scalar_tensor_tensor(
+                    out=gate_t[:, :, cols], in0=gate_t[:, :, cols], scalar=1.0, in1=gate_t[:, :, cols],
+                    op0=ALU.subtract, op1=ALU.mult,
+                )
+                nc.vector.scalar_tensor_tensor(
+                    out=flow_t[:, :, cols], in0=grad_t[:, :, cols], scalar=-1.0, in1=flow_t[:, :, cols],
+                    op0=ALU.mult, op1=ALU.mult,
+                )
+
+        def make_dz(i):
+            gate_t, grad_t, flow_t = inputs[i]
+            dz_g = grouped.tile([P, N_TILE, PACK], BF16, align_bytes=64)
+            nc.vector.tensor_tensor(
+                out=by_column(dz_g[:]), in0=by_token(gate_t[:]), in1=by_token(flow_t[:]), op=ALU.mult
+            )
+            dz_grouped[i] = dz_g
+
+        def quantise_dz(i):
+            c, n = units[i]
+            n_cols = slice(n * N_TILE, (n + 1) * N_TILE)
+            nc.vector.quantize_mx(
+                out=dz_codes[:, c, n_cols].bitcast(E5M2_X4), scales=dz_scales[:, c, n_cols],
+                in_=dz_grouped[i][:].rearrange("p w t -> p (w t)"),
+            )
+
+        def quantise_x(c):
+            nc.vector.quantize_mx(
+                out=x_codes[:, c, :].bitcast(E4M3_X4), scales=x_scales[:, c, :],
+                in_=x_grouped[c][:].rearrange("p w t -> p (w t)"),
             )
 
         def multiply(banks, c, n):
@@ -117,45 +155,29 @@ def tile_splatinformationflow_pb_v_kernel(
 
         for i in range(FETCH_AHEAD):
             fetch(i)
-        gate_slope(0)
 
-        for i, (c, n) in enumerate(units):
+        for i in range(len(units) + 1):
             if i + FETCH_AHEAD < len(units):
                 fetch(i + FETCH_AHEAD)
-            gate_t, grad_t, flow_t = inputs[i]
-            n_cols = slice(n * N_TILE, (n + 1) * N_TILE)
-            nc.vector.scalar_tensor_tensor(
-                out=flow_t[:], in0=grad_t[:], scalar=-1.0, in1=flow_t[:], op0=ALU.mult, op1=ALU.mult
-            )
-            dz_grouped = grouped.tile([P, N_TILE, PACK], BF16, align_bytes=64)
-            nc.vector.tensor_tensor(
-                out=by_column(dz_grouped[:]), in0=by_token(gate_t[:]), in1=by_token(flow_t[:]), op=ALU.mult
-            )
-            if i + 1 < len(units):
-                gate_slope(i + 1)
-            x_chunk = i - X_LAG
-            if 0 <= x_chunk < PASSES:
-                nc.vector.quantize_mx(
-                    out=x_codes[:, x_chunk, :].bitcast(E4M3_X4), scales=x_scales[:, x_chunk, :],
-                    in_=x_grouped[x_chunk][:].rearrange("p w t -> p (w t)"),
-                )
-            nc.vector.quantize_mx(
-                out=dz_codes[:, c, n_cols].bitcast(E5M2_X4), scales=dz_scales[:, c, n_cols],
-                in_=dz_grouped[:].rearrange("p w t -> p (w t)"),
-            )
-
-            if 0 <= x_chunk < PASSES:
-                multiply(round_0, x_chunk, 0)
-            if n == 1:
-                waiting.append(c)
-            if i == last_of_round_0:
+            if i < len(units):
+                make_factors(i)
+            if i >= 1:
+                quantise_dz(i - 1)
+                if units[i - 1][1] == 1:
+                    waiting.append(units[i - 1][0])
+            if 0 <= i - X_LAG < PASSES:
+                quantise_x(i - X_LAG)
+                multiply(round_0, i - X_LAG, 0)
+            if i - X_LAG == PASSES - 1:
                 for m in range(M_TILES):
                     store(round_0[m], m, 0, nc.scalar.copy)
                     round_1.append(psum.tile([M_TILE, N_TILE], F32, name="bank%d" % (M_TILES + m), tag="bank"))
-            if i >= last_of_round_0:
-                for ready in waiting:
-                    multiply(round_1, ready, 1)
+            if i - X_LAG >= PASSES - 1:
+                for c in waiting:
+                    multiply(round_1, c, 1)
                 waiting = []
+            if i < len(units):
+                make_dz(i)
 
         for m in range(M_TILES):
             store(round_1[m], m, 1, nc.scalar.copy if m % 2 == 0 else nc.vector.tensor_copy)

@@ -23,6 +23,7 @@ N_TILES = FEATURES // N_TILE
 LAST_GROUP = 2
 FETCH_AHEAD = 2
 X_LAG = 3
+X_FETCH_LAG = 2
 HEAD_PIECES = 2
 RUN = 4
 
@@ -86,12 +87,12 @@ def tile_splatinformationflow_pb_v_kernel(
                 nc.sync.dma_start(out=gate_t[:, :, cols], in_=chunk_of(gate, c)[:, :, dram_cols])
                 nc.sync.dma_start(out=grad_t[:, :, cols], in_=chunk_of(grad_out, c)[:, :, dram_cols])
                 nc.sync.dma_start(out=flow_t[:, :, cols], in_=chunk_of(flow, c)[:, :, dram_cols])
-            if 0 <= i - 1 < PASSES:
+            if 0 <= i - X_FETCH_LAG < PASSES:
                 x_t = x_stream.tile([P, PACK, FEATURES], BF16)
-                nc.sync.dma_start(out=x_t[:], in_=chunk_of(token_embeddings, i - 1))
+                nc.sync.dma_start(out=x_t[:], in_=chunk_of(token_embeddings, i - X_FETCH_LAG))
                 x_g = x_stream.tile([P, FEATURES, PACK], BF16, align_bytes=64)
                 nc.scalar.copy(out=by_column(x_g[:]), in_=by_token(x_t[:]))
-                x_grouped[i - 1] = x_g
+                x_grouped[i - X_FETCH_LAG] = x_g
 
         def make_factors(i):
             gate_t, grad_t, flow_t = inputs[i]

@@ -56,6 +56,7 @@ def tile_splatinformationflow_pb_v_kernel(
         ctx.enter_context(tc.manual_schedule())
         keep = ctx.enter_context(tc.tile_pool(name="keep", bufs=1))
         stream = ctx.enter_context(tc.tile_pool(name="stream", bufs=6))
+        grad_rows = ctx.enter_context(tc.tile_pool(name="grad_rows", bufs=PASSES))
         x_stream = ctx.enter_context(tc.tile_pool(name="x_stream", bufs=2))
         grouped = ctx.enter_context(tc.tile_pool(name="grouped", bufs=2))
         results = ctx.enter_context(tc.tile_pool(name="results", bufs=M_TILES))
@@ -67,6 +68,7 @@ def tile_splatinformationflow_pb_v_kernel(
         dz_scales = keep.tile([P, PASSES, FEATURES], U8, align_bytes=64)
 
         inputs = {}
+        grad_chunks = {}
         x_grouped = {}
         dz_grouped = {}
 
@@ -78,14 +80,22 @@ def tile_splatinformationflow_pb_v_kernel(
         def fetch(i):
             c, n = units[i]
             gate_t = stream.tile([P, PACK, N_TILE], F32)
-            grad_t = stream.tile([P, PACK, N_TILE], BF16)
             flow_t = stream.tile([P, PACK, N_TILE], F32)
+            whole_rows = c >= 1
+            first_of_chunk = c not in grad_chunks
+            if first_of_chunk:
+                grad_c = grad_rows.tile([P, PACK, FEATURES], BF16)
+                grad_chunks[c] = grad_c
+            grad_t = grad_chunks[c][:, :, n * N_TILE : (n + 1) * N_TILE]
             inputs[i] = (gate_t, grad_t, flow_t)
             for lo, hi in pieces_of(i):
                 cols = slice(lo, hi)
                 dram_cols = slice(n * N_TILE + lo, n * N_TILE + hi)
                 nc.sync.dma_start(out=gate_t[:, :, cols], in_=chunk_of(gate, c)[:, :, dram_cols])
-                nc.sync.dma_start(out=grad_t[:, :, cols], in_=chunk_of(grad_out, c)[:, :, dram_cols])
+                if not whole_rows:
+                    nc.sync.dma_start(out=grad_t[:, :, cols], in_=chunk_of(grad_out, c)[:, :, dram_cols])
+                elif first_of_chunk:
+                    nc.sync.dma_start(out=grad_chunks[c][:], in_=chunk_of(grad_out, c))
                 nc.sync.dma_start(out=flow_t[:, :, cols], in_=chunk_of(flow, c)[:, :, dram_cols])
             if 0 <= i - X_FETCH_LAG < PASSES:
                 x_t = x_stream.tile([P, PACK, FEATURES], BF16)

@@ -1,6 +1,7 @@
 from contextlib import ExitStack
 
 import concourse.mybir as mybir
+from concourse.masks import make_identity
 
 F32 = mybir.dt.float32
 BF16 = mybir.dt.bfloat16
@@ -9,6 +10,7 @@ U8 = mybir.dt.uint8
 E4M3_X4 = mybir.dt.float8_e4m3fn_x4
 E5M2_X4 = mybir.dt.float8_e5m2_x4
 ALU = mybir.AluOpType
+ACT = mybir.ActivationFunctionType
 
 P = 128
 PACK = 4
@@ -26,6 +28,10 @@ X_LAG = 3
 X_FETCH_LAG = 2
 HEAD_PIECES = 2
 RUN = 4
+STAGED = (1, 2, 3, 4, 5)
+STAGE_BANKS = 2
+ACC_BANKS = M_TILES - STAGE_BANKS
+POOL_COLS = 192
 
 FLOPS = 2 * TOKENS * FEATURES * FEATURES
 BYTES = TOKENS * FEATURES * (2 + 2 + 4 + 4) + FEATURES * FEATURES * 4
@@ -55,12 +61,18 @@ def tile_splatinformationflow_pb_v_kernel(
     with ExitStack() as ctx:
         ctx.enter_context(tc.manual_schedule())
         keep = ctx.enter_context(tc.tile_pool(name="keep", bufs=1))
-        stream = ctx.enter_context(tc.tile_pool(name="stream", bufs=6))
+        stream = ctx.enter_context(tc.tile_pool(name="stream", bufs=5))
+        factor = ctx.enter_context(tc.tile_pool(name="factor", bufs=1))
+        minus = ctx.enter_context(tc.tile_pool(name="minus", bufs=3))
         grad_rows = ctx.enter_context(tc.tile_pool(name="grad_rows", bufs=PASSES))
         x_stream = ctx.enter_context(tc.tile_pool(name="x_stream", bufs=2))
         grouped = ctx.enter_context(tc.tile_pool(name="grouped", bufs=2))
         results = ctx.enter_context(tc.tile_pool(name="results", bufs=M_TILES))
-        psum = ctx.enter_context(tc.psum_pool(name="psum", bufs=M_TILES))
+        psum = ctx.enter_context(tc.psum_pool(name="psum", bufs=ACC_BANKS))
+        psum_stage = ctx.enter_context(tc.psum_pool(name="psum_stage", bufs=STAGE_BANKS))
+
+        identity = keep.tile([P, P], BF16)
+        make_identity(nc, identity[:])
 
         x_codes = keep.tile([P, PASSES, FEATURES], U32, align_bytes=64)
         x_scales = keep.tile([P, PASSES, FEATURES], U8, align_bytes=64)
@@ -69,6 +81,9 @@ def tile_splatinformationflow_pb_v_kernel(
 
         inputs = {}
         grad_chunks = {}
+        gate_less_one = {}
+        gate_factor = {}
+        grad_staged = {}
         x_grouped = {}
         dz_grouped = {}
 
@@ -97,6 +112,10 @@ def tile_splatinformationflow_pb_v_kernel(
                 elif first_of_chunk:
                     nc.sync.dma_start(out=grad_chunks[c][:], in_=chunk_of(grad_out, c))
                 nc.sync.dma_start(out=flow_t[:, :, cols], in_=chunk_of(flow, c)[:, :, dram_cols])
+            if i in STAGED:
+                less_one = minus.tile([P, PACK, POOL_COLS], F32)
+                nc.scalar.activation(out=less_one[:], in_=gate_t[:, :, :POOL_COLS], func=ACT.Copy, bias=-1.0, scale=1.0)
+                gate_less_one[i] = less_one
             if 0 <= i - X_FETCH_LAG < PASSES:
                 x_t = x_stream.tile([P, PACK, FEATURES], BF16)
                 nc.sync.dma_start(out=x_t[:], in_=chunk_of(token_embeddings, i - X_FETCH_LAG))
@@ -104,12 +123,42 @@ def tile_splatinformationflow_pb_v_kernel(
                 nc.scalar.copy(out=by_column(x_g[:]), in_=by_token(x_t[:]))
                 x_grouped[i - X_FETCH_LAG] = x_g
 
+        def stage_grad(i):
+            gate_t, grad_t, flow_t = inputs[i]
+            halves = []
+            for h in range(STAGE_BANKS):
+                half = psum_stage.tile([P, PACK // STAGE_BANKS, N_TILE], BF16, name="grad%d_%d" % (i, h), tag="stage")
+                for j in range(PACK // STAGE_BANKS):
+                    nc.tensor.matmul(
+                        out=half[:, j, :], lhsT=identity[:], rhs=grad_t[:, h * (PACK // STAGE_BANKS) + j, :],
+                        start=True, stop=True,
+                    )
+                halves.append(half)
+            grad_staged[i] = halves
+
         def make_factors(i):
             gate_t, grad_t, flow_t = inputs[i]
+            a_t = factor.tile([P, PACK, N_TILE], F32)
+            gate_factor[i] = a_t
+            if i in STAGED:
+                nc.gpsimd.tensor_tensor(
+                    out=a_t[:, :, :POOL_COLS], in0=gate_t[:, :, :POOL_COLS], in1=gate_less_one[i][:], op=ALU.mult
+                )
+                rows = PACK // STAGE_BANKS
+                for h in range(STAGE_BANKS):
+                    nc.vector.scalar_tensor_tensor(
+                        out=flow_t[:, h * rows : (h + 1) * rows, :], in0=grad_staged[i][h][:], scalar=-1.0,
+                        in1=flow_t[:, h * rows : (h + 1) * rows, :], op0=ALU.mult, op1=ALU.mult,
+                    )
+                nc.vector.scalar_tensor_tensor(
+                    out=a_t[:, :, POOL_COLS:], in0=gate_t[:, :, POOL_COLS:], scalar=1.0, in1=gate_t[:, :, POOL_COLS:],
+                    op0=ALU.subtract, op1=ALU.mult,
+                )
+                return
             for lo, hi in pieces_of(i):
                 cols = slice(lo, hi)
                 nc.vector.scalar_tensor_tensor(
-                    out=gate_t[:, :, cols], in0=gate_t[:, :, cols], scalar=1.0, in1=gate_t[:, :, cols],
+                    out=a_t[:, :, cols], in0=gate_t[:, :, cols], scalar=1.0, in1=gate_t[:, :, cols],
                     op0=ALU.subtract, op1=ALU.mult,
                 )
                 nc.vector.scalar_tensor_tensor(
@@ -121,7 +170,7 @@ def tile_splatinformationflow_pb_v_kernel(
             gate_t, grad_t, flow_t = inputs[i]
             dz_g = grouped.tile([P, N_TILE, PACK], BF16, align_bytes=64)
             nc.vector.tensor_tensor(
-                out=by_column(dz_g[:]), in0=by_token(gate_t[:]), in1=by_token(flow_t[:]), op=ALU.mult
+                out=by_column(dz_g[:]), in0=by_token(gate_factor[i][:]), in1=by_token(flow_t[:]), op=ALU.mult
             )
             dz_grouped[i] = dz_g
 
@@ -139,9 +188,9 @@ def tile_splatinformationflow_pb_v_kernel(
                 in_=x_grouped[c][:].rearrange("p w t -> p (w t)"),
             )
 
-        def multiply(banks, c, n):
+        def multiply(banks, c, n, m_tiles):
             n_cols = slice(n * N_TILE, (n + 1) * N_TILE)
-            for m in range(M_TILES):
+            for m in m_tiles:
                 m_cols = slice(m * M_TILE, (m + 1) * M_TILE)
                 nc.tensor.matmul_mx(
                     out=banks[m][:],
@@ -160,7 +209,14 @@ def tile_splatinformationflow_pb_v_kernel(
                 out=out[m * M_TILE : (m + 1) * M_TILE, n * N_TILE : (n + 1) * N_TILE], in_=result[:]
             )
 
-        round_0 = [psum.tile([M_TILE, N_TILE], F32, name="bank%d" % m, tag="bank") for m in range(M_TILES)]
+        def bank_for(m, name):
+            pool, tag = (psum, "bank") if m < ACC_BANKS else (psum_stage, "stage")
+            return pool.tile([M_TILE, N_TILE], F32, name=name, tag=tag)
+
+        early = list(range(ACC_BANKS))
+        late = list(range(ACC_BANKS, M_TILES))
+        every = early + late
+        round_0 = [bank_for(m, "bank%d" % m) for m in early]
         round_1 = []
         waiting = []
 
@@ -172,23 +228,34 @@ def tile_splatinformationflow_pb_v_kernel(
                 fetch(i + FETCH_AHEAD)
             if i < len(units):
                 make_factors(i)
+            if i + 1 in STAGED:
+                stage_grad(i + 1)
             if i >= 1:
                 quantise_dz(i - 1)
                 if units[i - 1][1] == 1:
                     waiting.append(units[i - 1][0])
-            if 0 <= i - X_LAG < PASSES:
-                quantise_x(i - X_LAG)
-                multiply(round_0, i - X_LAG, 0)
-            if i - X_LAG == PASSES - 1:
-                for m in range(M_TILES):
+            c_x = i - X_LAG
+            if 0 <= c_x < PASSES:
+                quantise_x(c_x)
+                if i < max(STAGED):
+                    multiply(round_0, c_x, 0, early)
+                elif i == max(STAGED):
+                    multiply(round_0, c_x, 0, early)
+                    round_0.extend(bank_for(m, "bank%d" % m) for m in late)
+                    for c in range(c_x + 1):
+                        multiply(round_0, c, 0, late)
+                else:
+                    multiply(round_0, c_x, 0, every)
+            if c_x == PASSES - 1:
+                for m in every:
                     store(round_0[m], m, 0, nc.scalar.copy)
-                    round_1.append(psum.tile([M_TILE, N_TILE], F32, name="bank%d" % (M_TILES + m), tag="bank"))
-            if i - X_LAG >= PASSES - 1:
+                    round_1.append(bank_for(m, "bank%d" % (M_TILES + m)))
+            if c_x >= PASSES - 1:
                 for c in waiting:
-                    multiply(round_1, c, 1)
+                    multiply(round_1, c, 1, every)
                 waiting = []
             if i < len(units):
                 make_dz(i)
 
-        for m in range(M_TILES):
+        for m in every:
             store(round_1[m], m, 1, nc.scalar.copy if m % 2 == 0 else nc.vector.tensor_copy)

@@ -24,14 +24,16 @@ M_TILES = FEATURES // M_TILE
 N_TILES = FEATURES // N_TILE
 LAST_GROUP = 2
 FETCH_AHEAD = 2
-X_LAG = 3
-X_FETCH_LAG = 2
+X_BEHIND = (2, 3, 5, 5)
+X_STEP = (3, 4, 6, 6)
+CLOSING = 6
 HEAD_PIECES = 2
 RUN = 4
-STAGED = (1, 2, 3, 4, 5)
+STAGED = (1, 2, 3, 4)
 STAGE_BANKS = 2
 ACC_BANKS = M_TILES - STAGE_BANKS
 POOL_COLS = 192
+SHARED_COLS = 8
 
 FLOPS = 2 * TOKENS * FEATURES * FEATURES
 BYTES = TOKENS * FEATURES * (2 + 2 + 4 + 4) + FEATURES * FEATURES * 4
@@ -56,13 +58,14 @@ def tile_splatinformationflow_pb_v_kernel(
 
     groups = [[c] for c in range(PASSES - LAST_GROUP)] + [list(range(PASSES - LAST_GROUP, PASSES))]
     units = [(c, n) for group in groups for n in range(N_TILES) for c in group]
-    assert all(units.index((c, 0)) + 1 <= c + X_LAG for c in range(PASSES))
+    last = len(units) - 1
+    whole = slice(0, N_TILE)
 
     with ExitStack() as ctx:
         ctx.enter_context(tc.manual_schedule())
         keep = ctx.enter_context(tc.tile_pool(name="keep", bufs=1))
-        stream = ctx.enter_context(tc.tile_pool(name="stream", bufs=5))
-        factor = ctx.enter_context(tc.tile_pool(name="factor", bufs=1))
+        stream = ctx.enter_context(tc.tile_pool(name="stream", bufs=4))
+        factor = ctx.enter_context(tc.tile_pool(name="factor", bufs=2))
         minus = ctx.enter_context(tc.tile_pool(name="minus", bufs=3))
         grad_rows = ctx.enter_context(tc.tile_pool(name="grad_rows", bufs=PASSES))
         x_stream = ctx.enter_context(tc.tile_pool(name="x_stream", bufs=2))
@@ -84,13 +87,22 @@ def tile_splatinformationflow_pb_v_kernel(
         gate_less_one = {}
         gate_factor = {}
         grad_staged = {}
+        x_loaded = []
+        x_rows = {}
         x_grouped = {}
         dz_grouped = {}
 
         def pieces_of(i):
             pieces = HEAD_PIECES if i == 0 else 1
             width = N_TILE // pieces
-            return [(k * width, (k + 1) * width) for k in range(pieces)]
+            return [slice(k * width, (k + 1) * width) for k in range(pieces)]
+
+        def regroup_x():
+            for c in x_loaded:
+                x_g = x_stream.tile([P, FEATURES, PACK], BF16, align_bytes=64)
+                nc.scalar.copy(out=by_column(x_g[:]), in_=by_token(x_rows[c][:]))
+                x_grouped[c] = x_g
+            x_loaded.clear()
 
         def fetch(i):
             c, n = units[i]
@@ -103,9 +115,8 @@ def tile_splatinformationflow_pb_v_kernel(
                 grad_chunks[c] = grad_c
             grad_t = grad_chunks[c][:, :, n * N_TILE : (n + 1) * N_TILE]
             inputs[i] = (gate_t, grad_t, flow_t)
-            for lo, hi in pieces_of(i):
-                cols = slice(lo, hi)
-                dram_cols = slice(n * N_TILE + lo, n * N_TILE + hi)
+            for cols in pieces_of(i):
+                dram_cols = slice(n * N_TILE + cols.start, n * N_TILE + cols.stop)
                 nc.sync.dma_start(out=gate_t[:, :, cols], in_=chunk_of(gate, c)[:, :, dram_cols])
                 if not whole_rows:
                     nc.sync.dma_start(out=grad_t[:, :, cols], in_=chunk_of(grad_out, c)[:, :, dram_cols])
@@ -116,54 +127,55 @@ def tile_splatinformationflow_pb_v_kernel(
                 less_one = minus.tile([P, PACK, POOL_COLS], F32)
                 nc.scalar.activation(out=less_one[:], in_=gate_t[:, :, :POOL_COLS], func=ACT.Copy, bias=-1.0, scale=1.0)
                 gate_less_one[i] = less_one
-            if 0 <= i - X_FETCH_LAG < PASSES:
-                x_t = x_stream.tile([P, PACK, FEATURES], BF16)
-                nc.sync.dma_start(out=x_t[:], in_=chunk_of(token_embeddings, i - X_FETCH_LAG))
-                x_g = x_stream.tile([P, FEATURES, PACK], BF16, align_bytes=64)
-                nc.scalar.copy(out=by_column(x_g[:]), in_=by_token(x_t[:]))
-                x_grouped[i - X_FETCH_LAG] = x_g
+            regroup_x()
+            for c_x in range(PASSES):
+                if X_BEHIND[c_x] == i:
+                    x_t = x_stream.tile([P, PACK, FEATURES], BF16)
+                    nc.sync.dma_start(out=x_t[:], in_=chunk_of(token_embeddings, c_x))
+                    x_rows[c_x] = x_t
+                    x_loaded.append(c_x)
 
         def stage_grad(i):
             gate_t, grad_t, flow_t = inputs[i]
+            rows = PACK // STAGE_BANKS
             halves = []
             for h in range(STAGE_BANKS):
-                half = psum_stage.tile([P, PACK // STAGE_BANKS, N_TILE], BF16, name="grad%d_%d" % (i, h), tag="stage")
-                for j in range(PACK // STAGE_BANKS):
+                half = psum_stage.tile([P, rows, N_TILE], BF16, name="grad%d_%d" % (i, h), tag="stage")
+                for j in range(rows):
                     nc.tensor.matmul(
-                        out=half[:, j, :], lhsT=identity[:], rhs=grad_t[:, h * (PACK // STAGE_BANKS) + j, :],
-                        start=True, stop=True,
+                        out=half[:, j, :], lhsT=identity[:], rhs=grad_t[:, h * rows + j, :], start=True, stop=True
                     )
                 halves.append(half)
             grad_staged[i] = halves
 
-        def make_factors(i):
+        def make_gate_factor(i, cols):
             gate_t, grad_t, flow_t = inputs[i]
-            a_t = factor.tile([P, PACK, N_TILE], F32)
-            gate_factor[i] = a_t
-            if i in STAGED:
-                nc.gpsimd.tensor_tensor(
-                    out=a_t[:, :, :POOL_COLS], in0=gate_t[:, :, :POOL_COLS], in1=gate_less_one[i][:], op=ALU.mult
-                )
-                rows = PACK // STAGE_BANKS
-                for h in range(STAGE_BANKS):
-                    nc.vector.scalar_tensor_tensor(
-                        out=flow_t[:, h * rows : (h + 1) * rows, :], in0=grad_staged[i][h][:], scalar=-1.0,
-                        in1=flow_t[:, h * rows : (h + 1) * rows, :], op0=ALU.mult, op1=ALU.mult,
-                    )
+            if i not in gate_factor:
+                a_t = factor.tile([P, PACK, N_TILE], F32)
+                gate_factor[i] = a_t
+            nc.vector.scalar_tensor_tensor(
+                out=gate_factor[i][:, :, cols], in0=gate_t[:, :, cols], scalar=1.0, in1=gate_t[:, :, cols],
+                op0=ALU.subtract, op1=ALU.mult,
+            )
+
+        def make_flow_factor(i, cols):
+            gate_t, grad_t, flow_t = inputs[i]
+            nc.vector.scalar_tensor_tensor(
+                out=flow_t[:, :, cols], in0=grad_t[:, :, cols], scalar=-1.0, in1=flow_t[:, :, cols],
+                op0=ALU.mult, op1=ALU.mult,
+            )
+
+        def make_factors_staged(i):
+            gate_t, grad_t, flow_t = inputs[i]
+            make_gate_factor(i, slice(POOL_COLS - SHARED_COLS, N_TILE))
+            nc.gpsimd.tensor_tensor(
+                out=gate_factor[i][:, :, :POOL_COLS], in0=gate_t[:, :, :POOL_COLS], in1=gate_less_one[i][:], op=ALU.mult
+            )
+            rows = PACK // STAGE_BANKS
+            for h in range(STAGE_BANKS):
                 nc.vector.scalar_tensor_tensor(
-                    out=a_t[:, :, POOL_COLS:], in0=gate_t[:, :, POOL_COLS:], scalar=1.0, in1=gate_t[:, :, POOL_COLS:],
-                    op0=ALU.subtract, op1=ALU.mult,
-                )
-                return
-            for lo, hi in pieces_of(i):
-                cols = slice(lo, hi)
-                nc.vector.scalar_tensor_tensor(
-                    out=a_t[:, :, cols], in0=gate_t[:, :, cols], scalar=1.0, in1=gate_t[:, :, cols],
-                    op0=ALU.subtract, op1=ALU.mult,
-                )
-                nc.vector.scalar_tensor_tensor(
-                    out=flow_t[:, :, cols], in0=grad_t[:, :, cols], scalar=-1.0, in1=flow_t[:, :, cols],
-                    op0=ALU.mult, op1=ALU.mult,
+                    out=flow_t[:, h * rows : (h + 1) * rows, :], in0=grad_staged[i][h][:], scalar=-1.0,
+                    in1=flow_t[:, h * rows : (h + 1) * rows, :], op0=ALU.mult, op1=ALU.mult,
                 )
 
         def make_dz(i):
@@ -220,41 +232,61 @@ def tile_splatinformationflow_pb_v_kernel(
         round_1 = []
         waiting = []
 
+        def quantise_x_and_multiply(i, c):
+            quantise_x(c)
+            if i < max(STAGED):
+                multiply(round_0, c, 0, early)
+            elif i == max(STAGED):
+                multiply(round_0, c, 0, early)
+                round_0.extend(bank_for(m, "bank%d" % m) for m in late)
+                for c_done in range(c + 1):
+                    multiply(round_0, c_done, 0, late)
+            else:
+                multiply(round_0, c, 0, every)
+
         for i in range(FETCH_AHEAD):
             fetch(i)
 
         for i in range(len(units) + 1):
             if i + FETCH_AHEAD < len(units):
                 fetch(i + FETCH_AHEAD)
-            if i < len(units):
-                make_factors(i)
+            elif i + FETCH_AHEAD == len(units):
+                regroup_x()
+            x_now = [c for c in range(PASSES) if X_STEP[c] == i]
+            if i in STAGED:
+                make_factors_staged(i)
+            elif i < CLOSING:
+                for cols in pieces_of(i):
+                    make_gate_factor(i, cols)
+                    make_flow_factor(i, cols)
+            elif i == CLOSING:
+                make_gate_factor(i, whole)
+            elif i <= last:
+                make_flow_factor(i, whole)
             if i + 1 in STAGED:
                 stage_grad(i + 1)
             if i >= 1:
                 quantise_dz(i - 1)
                 if units[i - 1][1] == 1:
                     waiting.append(units[i - 1][0])
-            c_x = i - X_LAG
-            if 0 <= c_x < PASSES:
-                quantise_x(c_x)
-                if i < max(STAGED):
-                    multiply(round_0, c_x, 0, early)
-                elif i == max(STAGED):
-                    multiply(round_0, c_x, 0, early)
-                    round_0.extend(bank_for(m, "bank%d" % m) for m in late)
-                    for c in range(c_x + 1):
-                        multiply(round_0, c, 0, late)
-                else:
-                    multiply(round_0, c_x, 0, every)
-            if c_x == PASSES - 1:
+            if i < CLOSING:
+                for c in x_now:
+                    quantise_x_and_multiply(i, c)
+            if i == CLOSING:
+                quantise_x_and_multiply(i, x_now[0])
+                make_flow_factor(i, whole)
+                quantise_x_and_multiply(i, x_now[1])
                 for m in every:
                     store(round_0[m], m, 0, nc.scalar.copy)
                     round_1.append(bank_for(m, "bank%d" % (M_TILES + m)))
-            if c_x >= PASSES - 1:
+            if i >= CLOSING:
                 for c in waiting:
                     multiply(round_1, c, 1, every)
                 waiting = []
-            if i < len(units):
+            if i == CLOSING:
+                for later in range(i + 1, len(units)):
+                    make_gate_factor(later, whole)
+            if i <= last:
                 make_dz(i)
 
         for m in every:

@@ -24,12 +24,12 @@ M_TILES = FEATURES // M_TILE
 N_TILES = FEATURES // N_TILE
 LAST_GROUP = 2
 FETCH_AHEAD = 2
-X_BEHIND = (2, 3, 5, 5)
-X_STEP = (3, 4, 6, 6)
+X_BEHIND = (2, 4, 5, 5)
+X_STEP = (3, 5, 6, 6)
 CLOSING = 6
 HEAD_PIECES = 2
 RUN = 4
-STAGED = (1, 2, 3, 4)
+STAGED = (2, 3, 4, 5)
 STAGE_BANKS = 2
 ACC_BANKS = M_TILES - STAGE_BANKS
 POOL_COLS = 192
@@ -108,7 +108,7 @@ def tile_splatinformationflow_pb_v_kernel(
             c, n = units[i]
             gate_t = stream.tile([P, PACK, N_TILE], F32)
             flow_t = stream.tile([P, PACK, N_TILE], F32)
-            whole_rows = c >= 1
+            whole_rows = 1 <= c < PASSES - LAST_GROUP
             first_of_chunk = c not in grad_chunks
             if first_of_chunk:
                 grad_c = grad_rows.tile([P, PACK, FEATURES], BF16)
@@ -236,13 +236,12 @@ def tile_splatinformationflow_pb_v_kernel(
             quantise_x(c)
             if i < max(STAGED):
                 multiply(round_0, c, 0, early)
-            elif i == max(STAGED):
-                multiply(round_0, c, 0, early)
+                return
+            if len(round_0) < M_TILES:
                 round_0.extend(bank_for(m, "bank%d" % m) for m in late)
-                for c_done in range(c + 1):
+                for c_done in range(c):
                     multiply(round_0, c_done, 0, late)
-            else:
-                multiply(round_0, c, 0, every)
+            multiply(round_0, c, 0, every)
 
         for i in range(FETCH_AHEAD):
             fetch(i)

@@ -32,7 +32,7 @@ RUN = 4
 STAGED = (2, 3, 4, 5)
 STAGE_BANKS = 2
 ACC_BANKS = M_TILES - STAGE_BANKS
-POOL_COLS = 192
+POOL_COLS = 224
 SHARED_COLS = 8
 
 FLOPS = 2 * TOKENS * FEATURES * FEATURES
@@ -69,6 +69,7 @@ def tile_splatinformationflow_pb_v_kernel(
         minus = ctx.enter_context(tc.tile_pool(name="minus", bufs=3))
         grad_rows = ctx.enter_context(tc.tile_pool(name="grad_rows", bufs=PASSES))
         x_stream = ctx.enter_context(tc.tile_pool(name="x_stream", bufs=2))
+        x_landing = ctx.enter_context(tc.tile_pool(name="x_landing", bufs=3))
         grouped = ctx.enter_context(tc.tile_pool(name="grouped", bufs=2))
         results = ctx.enter_context(tc.tile_pool(name="results", bufs=M_TILES))
         psum = ctx.enter_context(tc.psum_pool(name="psum", bufs=ACC_BANKS))
@@ -130,7 +131,7 @@ def tile_splatinformationflow_pb_v_kernel(
             regroup_x()
             for c_x in range(PASSES):
                 if X_BEHIND[c_x] == i:
-                    x_t = x_stream.tile([P, PACK, FEATURES], BF16)
+                    x_t = x_landing.tile([P, PACK, FEATURES], BF16)
                     nc.sync.dma_start(out=x_t[:], in_=chunk_of(token_embeddings, c_x))
                     x_rows[c_x] = x_t
                     x_loaded.append(c_x)
@@ -279,8 +280,9 @@ def tile_splatinformationflow_pb_v_kernel(
                     store(round_0[m], m, 0, nc.scalar.copy)
                     round_1.append(bank_for(m, "bank%d" % (M_TILES + m)))
             if i >= CLOSING:
-                for c in waiting:
-                    multiply(round_1, c, 1, every)
+                for m in every:
+                    for c in waiting:
+                        multiply(round_1, c, 1, [m])
                 waiting = []
             if i == CLOSING:
                 for later in range(i + 1, len(units)):

@@ -59,7 +59,7 @@ def tile_splatinformationflow_pb_v_kernel(
     groups = [[c] for c in range(PASSES - LAST_GROUP)] + [list(range(PASSES - LAST_GROUP, PASSES))]
     units = [(c, n) for group in groups for n in range(N_TILES) for c in group]
     last = len(units) - 1
-    whole = slice(0, N_TILE)
+    whole = (slice(0, PACK), slice(0, N_TILE))
 
     with ExitStack() as ctx:
         ctx.enter_context(tc.manual_schedule())
@@ -95,8 +95,8 @@ def tile_splatinformationflow_pb_v_kernel(
 
         def pieces_of(i):
             pieces = HEAD_PIECES if i == 0 else 1
-            width = N_TILE // pieces
-            return [slice(k * width, (k + 1) * width) for k in range(pieces)]
+            height = PACK // pieces
+            return [(slice(k * height, (k + 1) * height), slice(0, N_TILE)) for k in range(pieces)]
 
         def regroup_x():
             for c in x_loaded:
@@ -116,14 +116,14 @@ def tile_splatinformationflow_pb_v_kernel(
                 grad_chunks[c] = grad_c
             grad_t = grad_chunks[c][:, :, n * N_TILE : (n + 1) * N_TILE]
             inputs[i] = (gate_t, grad_t, flow_t)
-            for cols in pieces_of(i):
+            for rows, cols in pieces_of(i):
                 dram_cols = slice(n * N_TILE + cols.start, n * N_TILE + cols.stop)
-                nc.sync.dma_start(out=gate_t[:, :, cols], in_=chunk_of(gate, c)[:, :, dram_cols])
+                nc.sync.dma_start(out=gate_t[:, rows, cols], in_=chunk_of(gate, c)[:, rows, dram_cols])
                 if not whole_rows:
-                    nc.sync.dma_start(out=grad_t[:, :, cols], in_=chunk_of(grad_out, c)[:, :, dram_cols])
+                    nc.sync.dma_start(out=grad_t[:, rows, cols], in_=chunk_of(grad_out, c)[:, rows, dram_cols])
                 elif first_of_chunk:
                     nc.sync.dma_start(out=grad_chunks[c][:], in_=chunk_of(grad_out, c))
-                nc.sync.dma_start(out=flow_t[:, :, cols], in_=chunk_of(flow, c)[:, :, dram_cols])
+                nc.sync.dma_start(out=flow_t[:, rows, cols], in_=chunk_of(flow, c)[:, rows, dram_cols])
             if i in STAGED:
                 less_one = minus.tile([P, PACK, POOL_COLS], F32)
                 nc.scalar.activation(out=less_one[:], in_=gate_t[:, :, :POOL_COLS], func=ACT.Copy, bias=-1.0, scale=1.0)
@@ -149,26 +149,28 @@ def tile_splatinformationflow_pb_v_kernel(
                 halves.append(half)
             grad_staged[i] = halves
 
-        def make_gate_factor(i, cols):
+        def make_gate_factor(i, piece):
             gate_t, grad_t, flow_t = inputs[i]
+            rows, cols = piece
             if i not in gate_factor:
                 a_t = factor.tile([P, PACK, N_TILE], F32)
                 gate_factor[i] = a_t
             nc.vector.scalar_tensor_tensor(
-                out=gate_factor[i][:, :, cols], in0=gate_t[:, :, cols], scalar=1.0, in1=gate_t[:, :, cols],
+                out=gate_factor[i][:, rows, cols], in0=gate_t[:, rows, cols], scalar=1.0, in1=gate_t[:, rows, cols],
                 op0=ALU.subtract, op1=ALU.mult,
             )
 
-        def make_flow_factor(i, cols):
+        def make_flow_factor(i, piece):
             gate_t, grad_t, flow_t = inputs[i]
+            rows, cols = piece
             nc.vector.scalar_tensor_tensor(
-                out=flow_t[:, :, cols], in0=grad_t[:, :, cols], scalar=-1.0, in1=flow_t[:, :, cols],
+                out=flow_t[:, rows, cols], in0=grad_t[:, rows, cols], scalar=-1.0, in1=flow_t[:, rows, cols],
                 op0=ALU.mult, op1=ALU.mult,
             )
 
         def make_factors_staged(i):
             gate_t, grad_t, flow_t = inputs[i]
-            make_gate_factor(i, slice(POOL_COLS - SHARED_COLS, N_TILE))
+            make_gate_factor(i, (slice(0, PACK), slice(POOL_COLS - SHARED_COLS, N_TILE)))
             nc.gpsimd.tensor_tensor(
                 out=gate_factor[i][:, :, :POOL_COLS], in0=gate_t[:, :, :POOL_COLS], in1=gate_less_one[i][:], op=ALU.mult
             )
@@ -256,9 +258,9 @@ def tile_splatinformationflow_pb_v_kernel(
             if i in STAGED:
                 make_factors_staged(i)
             elif i < CLOSING:
-                for cols in pieces_of(i):
-                    make_gate_factor(i, cols)
-                    make_flow_factor(i, cols)
+                for piece in pieces_of(i):
+                    make_gate_factor(i, piece)
+                    make_flow_factor(i, piece)
             elif i == CLOSING:
                 make_gate_factor(i, whole)
             elif i <= last:

from contextlib import ExitStack

import concourse.mybir as mybir
from concourse.masks import make_identity

F32 = mybir.dt.float32
BF16 = mybir.dt.bfloat16
U32 = mybir.dt.uint32
U8 = mybir.dt.uint8
E4M3_X4 = mybir.dt.float8_e4m3fn_x4
E5M2_X4 = mybir.dt.float8_e5m2_x4
ALU = mybir.AluOpType
ACT = mybir.ActivationFunctionType

P = 128
PACK = 4
K_PASS = P * PACK
TOKENS = 2048
FEATURES = 1024
PASSES = TOKENS // K_PASS
M_TILE = 128
N_TILE = 512
M_TILES = FEATURES // M_TILE
N_TILES = FEATURES // N_TILE
LAST_GROUP = 2
FETCH_AHEAD = 2
X_BEHIND = (2, 4, 5, 5)
X_STEP = (3, 5, 6, 6)
CLOSING = 6
HEAD_PIECES = 2
RUN = 4
STAGED = (2, 3, 4, 5)
STAGE_BANKS = 2
ACC_BANKS = M_TILES - STAGE_BANKS
POOL_COLS = 224
SHARED_COLS = 8

FLOPS = 2 * TOKENS * FEATURES * FEATURES
BYTES = TOKENS * FEATURES * (2 + 2 + 4 + 4) + FEATURES * FEATURES * 4


def by_token(rows_cols):
    return rows_cols.rearrange("p t (c i) -> p c t i", i=RUN)


def by_column(cols_rows):
    return cols_rows.rearrange("p (c i) t -> p c t i", i=RUN)


def tile_splatinformationflow_pb_v_kernel(
    tc, token_embeddings, splat_influences, decoded, gate_W, gate_b, flow, gate, grad_out, out
):
    nc = tc.nc

    def chunk_of(tensor, c):
        rows = tensor.rearrange("b s d -> (b s) d")[c * K_PASS : (c + 1) * K_PASS, :]
        return rows.rearrange("(p t) w -> p t w", t=PACK)

    groups = [[c] for c in range(PASSES - LAST_GROUP)] + [list(range(PASSES - LAST_GROUP, PASSES))]
    units = [(c, n) for group in groups for n in range(N_TILES) for c in group]
    last = len(units) - 1
    whole = (slice(0, PACK), slice(0, N_TILE))

    with ExitStack() as ctx:
        ctx.enter_context(tc.manual_schedule())
        keep = ctx.enter_context(tc.tile_pool(name="keep", bufs=1))
        stream = ctx.enter_context(tc.tile_pool(name="stream", bufs=4))
        factor = ctx.enter_context(tc.tile_pool(name="factor", bufs=2))
        minus = ctx.enter_context(tc.tile_pool(name="minus", bufs=3))
        grad_rows = ctx.enter_context(tc.tile_pool(name="grad_rows", bufs=PASSES))
        x_stream = ctx.enter_context(tc.tile_pool(name="x_stream", bufs=2))
        x_landing = ctx.enter_context(tc.tile_pool(name="x_landing", bufs=3))
        grouped = ctx.enter_context(tc.tile_pool(name="grouped", bufs=2))
        results = ctx.enter_context(tc.tile_pool(name="results", bufs=M_TILES))
        psum = ctx.enter_context(tc.psum_pool(name="psum", bufs=ACC_BANKS))
        psum_stage = ctx.enter_context(tc.psum_pool(name="psum_stage", bufs=STAGE_BANKS))

        identity = keep.tile([P, P], BF16)
        make_identity(nc, identity[:])

        x_codes = keep.tile([P, PASSES, FEATURES], U32, align_bytes=64)
        x_scales = keep.tile([P, PASSES, FEATURES], U8, align_bytes=64)
        dz_codes = keep.tile([P, PASSES, FEATURES], U32, align_bytes=64)
        dz_scales = keep.tile([P, PASSES, FEATURES], U8, align_bytes=64)

        inputs = {}
        grad_chunks = {}
        gate_less_one = {}
        gate_factor = {}
        grad_staged = {}
        x_loaded = []
        x_rows = {}
        x_grouped = {}
        dz_grouped = {}

        def pieces_of(i):
            pieces = HEAD_PIECES if i == 0 else 1
            height = PACK // pieces
            return [(slice(k * height, (k + 1) * height), slice(0, N_TILE)) for k in range(pieces)]

        def regroup_x():
            for c in x_loaded:
                x_g = x_stream.tile([P, FEATURES, PACK], BF16, align_bytes=64)
                nc.scalar.copy(out=by_column(x_g[:]), in_=by_token(x_rows[c][:]))
                x_grouped[c] = x_g
            x_loaded.clear()

        def fetch(i):
            c, n = units[i]
            gate_t = stream.tile([P, PACK, N_TILE], F32)
            flow_t = stream.tile([P, PACK, N_TILE], F32)
            whole_rows = 1 <= c < PASSES - LAST_GROUP
            first_of_chunk = c not in grad_chunks
            if first_of_chunk:
                grad_c = grad_rows.tile([P, PACK, FEATURES], BF16)
                grad_chunks[c] = grad_c
            grad_t = grad_chunks[c][:, :, n * N_TILE : (n + 1) * N_TILE]
            inputs[i] = (gate_t, grad_t, flow_t)
            for rows, cols in pieces_of(i):
                dram_cols = slice(n * N_TILE + cols.start, n * N_TILE + cols.stop)
                nc.sync.dma_start(out=gate_t[:, rows, cols], in_=chunk_of(gate, c)[:, rows, dram_cols])
                if not whole_rows:
                    nc.sync.dma_start(out=grad_t[:, rows, cols], in_=chunk_of(grad_out, c)[:, rows, dram_cols])
                elif first_of_chunk:
                    nc.sync.dma_start(out=grad_chunks[c][:], in_=chunk_of(grad_out, c))
                nc.sync.dma_start(out=flow_t[:, rows, cols], in_=chunk_of(flow, c)[:, rows, dram_cols])
            if i in STAGED:
                less_one = minus.tile([P, PACK, POOL_COLS], F32)
                nc.scalar.activation(out=less_one[:], in_=gate_t[:, :, :POOL_COLS], func=ACT.Copy, bias=-1.0, scale=1.0)
                gate_less_one[i] = less_one
            regroup_x()
            for c_x in range(PASSES):
                if X_BEHIND[c_x] == i:
                    x_t = x_landing.tile([P, PACK, FEATURES], BF16)
                    nc.sync.dma_start(out=x_t[:], in_=chunk_of(token_embeddings, c_x))
                    x_rows[c_x] = x_t
                    x_loaded.append(c_x)

        def stage_grad(i):
            gate_t, grad_t, flow_t = inputs[i]
            rows = PACK // STAGE_BANKS
            halves = []
            for h in range(STAGE_BANKS):
                half = psum_stage.tile([P, rows, N_TILE], BF16, name="grad%d_%d" % (i, h), tag="stage")
                for j in range(rows):
                    nc.tensor.matmul(
                        out=half[:, j, :], lhsT=identity[:], rhs=grad_t[:, h * rows + j, :], start=True, stop=True
                    )
                halves.append(half)
            grad_staged[i] = halves

        def make_gate_factor(i, piece):
            gate_t, grad_t, flow_t = inputs[i]
            rows, cols = piece
            if i not in gate_factor:
                a_t = factor.tile([P, PACK, N_TILE], F32)
                gate_factor[i] = a_t
            nc.vector.scalar_tensor_tensor(
                out=gate_factor[i][:, rows, cols], in0=gate_t[:, rows, cols], scalar=1.0, in1=gate_t[:, rows, cols],
                op0=ALU.subtract, op1=ALU.mult,
            )

        def make_flow_factor(i, piece):
            gate_t, grad_t, flow_t = inputs[i]
            rows, cols = piece
            nc.vector.scalar_tensor_tensor(
                out=flow_t[:, rows, cols], in0=grad_t[:, rows, cols], scalar=-1.0, in1=flow_t[:, rows, cols],
                op0=ALU.mult, op1=ALU.mult,
            )

        def make_factors_staged(i):
            gate_t, grad_t, flow_t = inputs[i]
            make_gate_factor(i, (slice(0, PACK), slice(POOL_COLS - SHARED_COLS, N_TILE)))
            nc.gpsimd.tensor_tensor(
                out=gate_factor[i][:, :, :POOL_COLS], in0=gate_t[:, :, :POOL_COLS], in1=gate_less_one[i][:], op=ALU.mult
            )
            rows = PACK // STAGE_BANKS
            for h in range(STAGE_BANKS):
                nc.vector.scalar_tensor_tensor(
                    out=flow_t[:, h * rows : (h + 1) * rows, :], in0=grad_staged[i][h][:], scalar=-1.0,
                    in1=flow_t[:, h * rows : (h + 1) * rows, :], op0=ALU.mult, op1=ALU.mult,
                )

        def make_dz(i):
            gate_t, grad_t, flow_t = inputs[i]
            dz_g = grouped.tile([P, N_TILE, PACK], BF16, align_bytes=64)
            nc.vector.tensor_tensor(
                out=by_column(dz_g[:]), in0=by_token(gate_factor[i][:]), in1=by_token(flow_t[:]), op=ALU.mult
            )
            dz_grouped[i] = dz_g

        def quantise_dz(i):
            c, n = units[i]
            n_cols = slice(n * N_TILE, (n + 1) * N_TILE)
            nc.vector.quantize_mx(
                out=dz_codes[:, c, n_cols].bitcast(E5M2_X4), scales=dz_scales[:, c, n_cols],
                in_=dz_grouped[i][:].rearrange("p w t -> p (w t)"),
            )

        def quantise_x(c):
            nc.vector.quantize_mx(
                out=x_codes[:, c, :].bitcast(E4M3_X4), scales=x_scales[:, c, :],
                in_=x_grouped[c][:].rearrange("p w t -> p (w t)"),
            )

        def multiply(banks, c, n, m_tiles):
            n_cols = slice(n * N_TILE, (n + 1) * N_TILE)
            for m in m_tiles:
                m_cols = slice(m * M_TILE, (m + 1) * M_TILE)
                nc.tensor.matmul_mx(
                    out=banks[m][:],
                    lhsT=x_codes[:, c, m_cols].bitcast(E4M3_X4),
                    lhsT_scale=x_scales[:, c, m_cols],
                    rhs=dz_codes[:, c, n_cols].bitcast(E5M2_X4),
                    rhs_scale=dz_scales[:, c, n_cols],
                    start=(c == 0),
                    stop=(c == PASSES - 1),
                )

        def store(bank, m, n, copy):
            result = results.tile([M_TILE, N_TILE], F32)
            copy(out=result[:], in_=bank[:])
            nc.sync.dma_start(
                out=out[m * M_TILE : (m + 1) * M_TILE, n * N_TILE : (n + 1) * N_TILE], in_=result[:]
            )

        def bank_for(m, name):
            pool, tag = (psum, "bank") if m < ACC_BANKS else (psum_stage, "stage")
            return pool.tile([M_TILE, N_TILE], F32, name=name, tag=tag)

        early = list(range(ACC_BANKS))
        late = list(range(ACC_BANKS, M_TILES))
        every = early + late
        round_0 = [bank_for(m, "bank%d" % m) for m in early]
        round_1 = []
        waiting = []

        def quantise_x_and_multiply(i, c):
            quantise_x(c)
            if i < max(STAGED):
                multiply(round_0, c, 0, early)
                return
            if len(round_0) < M_TILES:
                round_0.extend(bank_for(m, "bank%d" % m) for m in late)
                for c_done in range(c):
                    multiply(round_0, c_done, 0, late)
            multiply(round_0, c, 0, every)

        for i in range(FETCH_AHEAD):
            fetch(i)

        for i in range(len(units) + 1):
            if i + FETCH_AHEAD < len(units):
                fetch(i + FETCH_AHEAD)
            elif i + FETCH_AHEAD == len(units):
                regroup_x()
            x_now = [c for c in range(PASSES) if X_STEP[c] == i]
            if i in STAGED:
                make_factors_staged(i)
            elif i < CLOSING:
                for piece in pieces_of(i):
                    make_gate_factor(i, piece)
                    make_flow_factor(i, piece)
            elif i == CLOSING:
                make_gate_factor(i, whole)
            elif i <= last:
                make_flow_factor(i, whole)
            if i + 1 in STAGED:
                stage_grad(i + 1)
            if i >= 1:
                quantise_dz(i - 1)
                if units[i - 1][1] == 1:
                    waiting.append(units[i - 1][0])
            if i < CLOSING:
                for c in x_now:
                    quantise_x_and_multiply(i, c)
            if i == CLOSING:
                quantise_x_and_multiply(i, x_now[0])
                make_flow_factor(i, whole)
                quantise_x_and_multiply(i, x_now[1])
                for m in every:
                    store(round_0[m], m, 0, nc.scalar.copy)
                    round_1.append(bank_for(m, "bank%d" % (M_TILES + m)))
            if i >= CLOSING:
                for m in every:
                    for c in waiting:
                        multiply(round_1, c, 1, [m])
                waiting = []
            if i == CLOSING:
                for later in range(i + 1, len(units)):
                    make_gate_factor(later, whole)
            if i <= last:
                make_dz(i)

        for m in every:
            store(round_1[m], m, 1, nc.scalar.copy if m % 2 == 0 else nc.vector.tensor_copy)
